import numpy as np
import ml_dtypes


BF16 = ml_dtypes.bfloat16


def bf(x):
    return np.asarray(x, np.float32).astype(BF16)


def f64(x):
    return np.asarray(x).astype(np.float64)


E2M1 = np.array([0.0, 0.5, 1.0, 1.5, 2.0, 3.0, 4.0, 6.0, -0.0, -0.5, -1.0, -1.5, -2.0, -3.0, -4.0, -6.0])


def pack_weight(w, fmt):
    k, n = w.shape
    w = f64(bf(w)).reshape(k // 32, 32, n)
    amax = np.abs(w).max(1)
    if fmt == "e4m3":
        byte = np.frexp(amax)[1] - 1 + 127 - 7
    else:
        mant, ex = np.frexp(amax / 6.0)
        byte = np.where(mant > 0.5, ex, ex - 1) + 127
    byte = np.clip(np.where(amax > 0, byte, 1), 1, 254)
    scaled = (w * np.exp2(127.0 - byte)[:, None, :]).reshape(k, n).astype(np.float32)
    by_word = np.ascontiguousarray(scaled.reshape(k // 512, 128, 4, n).transpose(0, 1, 3, 2))
    if fmt == "e4m3":
        words = by_word.astype(ml_dtypes.float8_e4m3fn).view(np.uint8)
    else:
        c = by_word.astype(ml_dtypes.float4_e2m1fn).view(np.uint8) & 0xF
        words = c[..., 0::2] | (c[..., 1::2] << 4)
    return np.ascontiguousarray(words), np.ascontiguousarray(byte.astype(np.uint8).reshape(k // 512, 16, n))


def unpack_weight(words, scales, fmt):
    g, p, n, _ = words.shape
    if fmt == "e4m3":
        vals = np.ascontiguousarray(words).view(ml_dtypes.float8_e4m3fn).astype(np.float64)
    else:
        nib = np.empty((g, p, n, 4), np.uint8)
        nib[..., 0::2] = words & 0xF
        nib[..., 1::2] = words >> 4
        vals = E2M1[nib]
    vals = vals * np.repeat(np.exp2(scales.astype(np.float64) - 127.0), 8, axis=1)[..., None]
    return vals.transpose(0, 1, 3, 2).reshape(g * 512, n)

def pack4(w):
    words, scales = pack_weight(w, "e2m1")
    return words.reshape(words.shape[0], 128, -1), scales


def unpack4(words, scales):
    return unpack_weight(words.reshape(words.shape[0], 128, -1, 2), scales, "e2m1")


def kspread(k):
    return np.exp2(np.repeat(np.random.randint(-6, 7, k // 32), 32).astype(np.float64))


B, N, DIM, HEADS, DIM_HEAD = 2, 256, 2048, 16, 64
INNER = HEADS * DIM_HEAD


def setup_inputs():
    s = kspread(DIM)
    x = np.random.standard_normal((B, N, DIM)) * s
    x_words, x_scales = pack4(np.ascontiguousarray(x.reshape(B * N, DIM).T))
    w = np.random.standard_normal((3 * INNER, DIM)) / np.sqrt(DIM) / s[None, :]
    words, scales = pack4(np.ascontiguousarray(w.T))
    return {"x_words": x_words, "x_scales": x_scales, "W_words": words, "W_scales": scales}


def reference(x_words, x_scales, W_words, W_scales):
    b, n = B, N
    x = unpack4(x_words, x_scales).T.reshape(B, N, DIM)
    qkv = x @ unpack4(W_words, W_scales)
    q, k, v = np.split(qkv, 3, axis=-1)

    def to_heads(t):
        return t.reshape(b, n, HEADS, DIM_HEAD).transpose(0, 2, 1, 3)

    return to_heads(q), to_heads(k), to_heads(v)

@@ -1,0 +1,157 @@
+from contextlib import ExitStack
+
+import concourse.mybir as mybir
+
+F32 = mybir.dt.float32
+BF16 = mybir.dt.bfloat16
+I32 = mybir.dt.int32
+U8 = mybir.dt.uint8
+E2M1X4 = mybir.dt.float4_e2m1fn_x4
+
+BATCH, POSITIONS, DIM, HEADS, DIM_HEAD = 2, 256, 2048, 16, 64
+TOKENS = BATCH * POSITIONS
+INNER = HEADS * DIM_HEAD
+P = 128
+PASSES = DIM // 512
+SETS = TOKENS // P
+WARM_UP = 9
+
+FLOPS = 2 * TOKENS * DIM * 3 * INNER
+
+
+def tile_get_qkv_kernel(tc, x_words, x_scales, w_words, w_scales, out_0, out_1, out_2):
+    nc = tc.nc
+    outs = (out_0, out_1, out_2)
+
+    with ExitStack() as ctx:
+        keep = ctx.enter_context(tc.tile_pool(name="keep", bufs=1))
+        results = ctx.enter_context(tc.tile_pool(name="results", bufs=4))
+        psum = ctx.enter_context(tc.psum_pool(name="psum", bufs=1))
+        ctx.enter_context(tc.manual_schedule())
+
+        zeros = keep.tile([P, 512], BF16, name="zeros", align_bytes=256)
+        scratch = keep.tile([P, 2], BF16, name="scratch", align_bytes=256)
+        x_raw = keep.tile([P, PASSES, 2 * TOKENS], U8, name="x_raw", align_bytes=256)
+        xs_raw = keep.tile([P, PASSES, TOKENS], U8, name="xs_raw", align_bytes=256)
+        x_codes = [keep.tile([P, SETS, 2 * P], U8, name="x_codes%d" % g, align_bytes=256) for g in range(PASSES)]
+        x_planes = [keep.tile([P, SETS, P], U8, name="x_planes%d" % g, align_bytes=256) for g in range(PASSES)]
+        w_codes = [keep.tile([P, PASSES, 2 * INNER], U8, name="w_codes%d" % i, align_bytes=256) for i in range(3)]
+        w_planes = [keep.tile([P, PASSES, INNER], U8, name="w_planes%d" % i, align_bytes=256) for i in range(3)]
+
+        def zero(engine, ap):
+            engine.memset(ap.bitcast(I32), 0)
+
+        def load_x(g0, g1):
+            nc.sync.dma_start(
+                out=x_raw[:, g0:g1, :].bitcast(I32), in_=x_words[g0:g1].rearrange("g p c -> p g c").bitcast(I32)
+            )
+
+        def load_w(i, g0, g1):
+            cols = slice(2 * INNER * i, 2 * INNER * (i + 1))
+            nc.sync.dma_start(
+                out=w_codes[i][:, g0:g1, :].bitcast(I32),
+                in_=w_words[g0:g1, :, cols].rearrange("g p c -> p g c").bitcast(I32),
+            )
+
+        def load_planes(planes, scales, g0, g1, c0, c1):
+            for quarter in range(4):
+                rows = slice(4 * quarter, 4 * quarter + 4)
+                nc.sync.dma_start(
+                    out=planes[32 * quarter : 32 * quarter + 4, g0:g1, :].bitcast(I32),
+                    in_=scales[g0:g1, rows, c0:c1].rearrange("g r c -> r g c").bitcast(I32),
+                )
+
+        def permute_codes(g):
+            nc.vector.tensor_copy(
+                out=x_codes[g][:].rearrange("p j (q b e) -> p j q b e", b=BATCH, e=2),
+                in_=x_raw[:, g, :].rearrange("p (b q j e) -> p j q b e", b=BATCH, j=SETS, e=2),
+            )
+
+        def permute_planes(g):
+            nc.vector.tensor_copy(
+                out=x_planes[g][:].rearrange("p j (q b) -> p j q b", b=BATCH),
+                in_=xs_raw[:, g, :].rearrange("p (b q j) -> p j q b", b=BATCH, j=SETS),
+            )
+
+        zero(nc.vector, xs_raw[:])
+        zero(nc.vector, w_planes[0][:, 0, :])
+        nc.gpsimd.memset(zeros[:], 0.0)
+        zero(nc.gpsimd, w_planes[0][:, 1:PASSES, :])
+        zero(nc.gpsimd, w_planes[1][:])
+        zero(nc.gpsimd, w_planes[2][:])
+        nc.scalar.copy(scratch[:], zeros[:, 0:2])
+
+        load_x(0, 1)
+        load_w(0, 0, 1)
+        load_planes(xs_raw, x_scales, 0, PASSES, 0, TOKENS)
+        load_planes(w_planes[0], w_scales, 0, 1, 0, INNER)
+        load_x(1, PASSES)
+        load_w(0, 1, 2)
+        load_planes(w_planes[0], w_scales, 1, PASSES, 0, INNER)
+        load_w(0, 2, PASSES)
+        for i in (1, 2):
+            load_w(i, 0, 2)
+            load_w(i, 2, PASSES)
+            load_planes(w_planes[i], w_scales, 0, PASSES, INNER * i, INNER * (i + 1))
+
+        for g in range(PASSES):
+            permute_codes(g)
+            permute_planes(g)
+
+        def bank(index):
+            acc = psum.tile([P, 512], F32, name="acc%d" % index)
+            return acc
+
+        warm = bank(7)
+        for n in range(WARM_UP):
+            nc.tensor.matmul(warm[:], lhsT=zeros[:, 0:P], rhs=zeros[:], start=True, stop=True)
+
+        def multiply(acc, i, c0, width, j, g):
+            nc.tensor.matmul_mx(
+                out=acc[:, 0:width],
+                lhsT=x_codes[g][:, j, :].bitcast(E2M1X4),
+                lhsT_scale=x_planes[g][:, j, :],
+                rhs=w_codes[i][:, g, 2 * c0 : 2 * (c0 + width)].bitcast(E2M1X4),
+                rhs_scale=w_planes[i][:, g, c0 : c0 + width],
+                start=(g == 0),
+                stop=(g == PASSES - 1),
+            )
+
+        def result_tile(width):
+            result = results.tile([P, width // DIM_HEAD, SETS, DIM_HEAD], F32, name="result%d" % width)
+            return result
+
+        def drain(copy, result, acc, width, j):
+            copy(out=result[:, :, j, :], in_=acc[:, 0:width].rearrange("p (h d) -> p h d", d=DIM_HEAD))
+
+        def store(result, i, c0, width):
+            heads = slice(c0 // DIM_HEAD, (c0 + width) // DIM_HEAD)
+            for b in range(BATCH):
+                nc.sync.dma_start(
+                    out=outs[i][b, heads, :, :].rearrange("h (q j) d -> q h (j d)", j=SETS),
+                    in_=result[b:P:BATCH, :, :, :].rearrange("q h j d -> q h (j d)"),
+                )
+
+        vector_copy = nc.vector.tensor_copy
+        scalar_copy = nc.scalar.copy
+
+        first = [(0, [bank(j) for j in range(SETS)]), (512, [bank(SETS + j) for j in range(SETS)])]
+        for half, g in ((0, 0), (1, 0), (0, 1), (1, 1), (0, 2), (0, 3), (1, 2), (1, 3)):
+            c0, accs = first[half]
+            for j in range(SETS):
+                multiply(accs[j], 0, c0, 512, j, g)
+        for (c0, accs), copy in zip(first, (scalar_copy, vector_copy)):
+            result = result_tile(512)
+            for j in range(SETS):
+                drain(copy, result, accs[j], 512, j)
+            store(result, 0, c0, 512)
+
+        blocks = [(1, 0, 512), (1, 512, 512), (2, 0, 512), (2, 512, 256), (2, 768, 128), (2, 896, 128)]
+        for n, (i, c0, width) in enumerate(blocks):
+            result = result_tile(width)
+            for j in range(SETS):
+                acc = bank(SETS * (n % 2) + j)
+                for g in range(PASSES):
+                    multiply(acc, i, c0, width, j, g)
+                drain((scalar_copy, vector_copy)[n % 2], result, acc, width, j)
+            store(result, i, c0, width)

@@ -53,6 +53,13 @@ def tile_get_qkv_kernel(tc, x_words, x_scales, w_words, w_scales, out_0, out_1, 
                 in_=w_words[g0:g1, :, cols].rearrange("g p c -> p g c").bitcast(I32),
             )
 
+        def load_planes_by_r(planes, scales, g0, g1, c0, c1):
+            for r in range(4):
+                nc.sync.dma_start(
+                    out=planes[r:P:32, g0:g1, :].bitcast(I32),
+                    in_=scales[g0:g1, r:16:4, c0:c1].rearrange("g r c -> r g c").bitcast(I32),
+                )
+
         def load_planes(planes, scales, g0, g1, c0, c1):
             for quarter in range(4):
                 rows = slice(4 * quarter, 4 * quarter + 4)
@@ -78,7 +85,6 @@ def tile_get_qkv_kernel(tc, x_words, x_scales, w_words, w_scales, out_0, out_1, 
         nc.gpsimd.memset(zeros[:], 0.0)
         zero(nc.gpsimd, w_planes[0][:, 1:PASSES, :])
         zero(nc.gpsimd, w_planes[1][:])
-        zero(nc.gpsimd, w_planes[2][:])
         nc.scalar.copy(scratch[:], zeros[:, 0:2])
 
         load_x(0, 1)
@@ -89,14 +95,15 @@ def tile_get_qkv_kernel(tc, x_words, x_scales, w_words, w_scales, out_0, out_1, 
         load_w(0, 1, 2)
         load_planes(w_planes[0], w_scales, 1, PASSES, 0, INNER)
         load_w(0, 2, PASSES)
-        for i in (1, 2):
-            load_w(i, 0, 2)
-            load_w(i, 2, PASSES)
-            load_planes(w_planes[i], w_scales, 0, PASSES, INNER * i, INNER * (i + 1))
+        load_w(1, 0, 2)
+        load_planes_by_r(w_planes[1], w_scales, 0, PASSES, INNER, 2 * INNER)
+        load_w(1, 2, PASSES)
+        load_w(2, 0, PASSES)
 
         for g in range(PASSES):
             permute_codes(g)
             permute_planes(g)
+        zero(nc.vector, w_planes[2][:])
 
         def bank(index):
             acc = psum.tile([P, 512], F32, name="acc%d" % index)
@@ -136,7 +143,7 @@ def tile_get_qkv_kernel(tc, x_words, x_scales, w_words, w_scales, out_0, out_1, 
         scalar_copy = nc.scalar.copy
 
         first = [(0, [bank(j) for j in range(SETS)]), (512, [bank(SETS + j) for j in range(SETS)])]
-        for half, g in ((0, 0), (1, 0), (0, 1), (1, 1), (0, 2), (0, 3), (1, 2), (1, 3)):
+        for half, g in ((0, 0), (1, 0), (0, 1), (1, 1), (0, 2), (1, 2), (0, 3), (1, 3)):
             c0, accs = first[half]
             for j in range(SETS):
                 multiply(accs[j], 0, c0, 512, j, g)
@@ -145,6 +152,7 @@ def tile_get_qkv_kernel(tc, x_words, x_scales, w_words, w_scales, out_0, out_1, 
             for j in range(SETS):
                 drain(copy, result, accs[j], 512, j)
             store(result, 0, c0, 512)
+        load_planes_by_r(w_planes[2], w_scales, 0, PASSES, 2 * INNER, 3 * INNER)
 
         blocks = [(1, 0, 512), (1, 512, 512), (2, 0, 512), (2, 512, 256), (2, 768, 128), (2, 896, 128)]
         for n, (i, c0, width) in enumerate(blocks):

@@ -36,6 +36,7 @@ def tile_get_qkv_kernel(tc, x_words, x_scales, w_words, w_scales, out_0, out_1, 
         x_codes = [keep.tile([P, SETS, 2 * P], U8, name="x_codes%d" % g, align_bytes=256) for g in range(PASSES)]
         x_planes = [keep.tile([P, SETS, P], U8, name="x_planes%d" % g, align_bytes=256) for g in range(PASSES)]
         w_codes = [keep.tile([P, PASSES, 2 * INNER], U8, name="w_codes%d" % i, align_bytes=256) for i in range(3)]
+        w_first_plane = keep.tile([P, 1, INNER], U8, name="w_first_plane", align_bytes=256)
         w_planes = [keep.tile([P, PASSES, INNER], U8, name="w_planes%d" % i, align_bytes=256) for i in range(3)]
 
         def zero(engine, ap):
@@ -46,26 +47,18 @@ def tile_get_qkv_kernel(tc, x_words, x_scales, w_words, w_scales, out_0, out_1, 
                 out=x_raw[:, g0:g1, :].bitcast(I32), in_=x_words[g0:g1].rearrange("g p c -> p g c").bitcast(I32)
             )
 
-        def load_w(i, g0, g1):
-            cols = slice(2 * INNER * i, 2 * INNER * (i + 1))
+        def load_w(i, g0, g1, c0=0, c1=INNER):
+            cols = slice(2 * (INNER * i + c0), 2 * (INNER * i + c1))
             nc.sync.dma_start(
-                out=w_codes[i][:, g0:g1, :].bitcast(I32),
+                out=w_codes[i][:, g0:g1, 2 * c0 : 2 * c1].bitcast(I32),
                 in_=w_words[g0:g1, :, cols].rearrange("g p c -> p g c").bitcast(I32),
             )
 
-        def load_planes_by_r(planes, scales, g0, g1, c0, c1):
-            for r in range(4):
+        def load_planes(planes, scales, g0, g1, c0, c1, rows=(0, 1, 2, 3)):
+            for r in rows:
                 nc.sync.dma_start(
                     out=planes[r:P:32, g0:g1, :].bitcast(I32),
                     in_=scales[g0:g1, r:16:4, c0:c1].rearrange("g r c -> r g c").bitcast(I32),
-                )
-
-        def load_planes(planes, scales, g0, g1, c0, c1):
-            for quarter in range(4):
-                rows = slice(4 * quarter, 4 * quarter + 4)
-                nc.sync.dma_start(
-                    out=planes[32 * quarter : 32 * quarter + 4, g0:g1, :].bitcast(I32),
-                    in_=scales[g0:g1, rows, c0:c1].rearrange("g r c -> r g c").bitcast(I32),
                 )
 
         def permute_codes(g):
@@ -80,30 +73,32 @@ def tile_get_qkv_kernel(tc, x_words, x_scales, w_words, w_scales, out_0, out_1, 
                 in_=xs_raw[:, g, :].rearrange("p (b q j) -> p j q b", b=BATCH, j=SETS),
             )
 
-        zero(nc.vector, xs_raw[:])
-        zero(nc.vector, w_planes[0][:, 0, :])
-        nc.gpsimd.memset(zeros[:], 0.0)
-        zero(nc.gpsimd, w_planes[0][:, 1:PASSES, :])
+        zero(nc.gpsimd, w_first_plane[:])
+        zero(nc.gpsimd, xs_raw[:])
+        nc.vector.memset(zeros[:].bitcast(I32), 0)
+        zero(nc.vector, w_planes[0][:, 1:PASSES, :])
         zero(nc.gpsimd, w_planes[1][:])
+        zero(nc.gpsimd, w_planes[2][:])
         nc.scalar.copy(scratch[:], zeros[:, 0:2])
 
+        load_planes(w_first_plane, w_scales, 0, 1, 0, INNER, (0, 1))
         load_x(0, 1)
+        load_planes(xs_raw, x_scales, 0, PASSES, 0, TOKENS, (0, 1, 2, 3))
+        load_planes(w_first_plane, w_scales, 0, 1, 0, INNER, (2, 3))
         load_w(0, 0, 1)
-        load_planes(xs_raw, x_scales, 0, PASSES, 0, TOKENS)
-        load_planes(w_planes[0], w_scales, 0, 1, 0, INNER)
-        load_x(1, PASSES)
+        load_x(1, 2)
         load_w(0, 1, 2)
         load_planes(w_planes[0], w_scales, 1, PASSES, 0, INNER)
+        load_x(2, PASSES)
         load_w(0, 2, PASSES)
-        load_w(1, 0, 2)
-        load_planes_by_r(w_planes[1], w_scales, 0, PASSES, INNER, 2 * INNER)
-        load_w(1, 2, PASSES)
-        load_w(2, 0, PASSES)
+        load_planes(w_planes[1], w_scales, 0, PASSES, INNER, 2 * INNER)
+        load_w(1, 0, PASSES)
+        load_planes(w_planes[2], w_scales, 0, PASSES, 2 * INNER, 3 * INNER)
+        load_w(2, 0, 2)
 
         for g in range(PASSES):
             permute_codes(g)
             permute_planes(g)
-        zero(nc.vector, w_planes[2][:])
 
         def bank(index):
             acc = psum.tile([P, 512], F32, name="acc%d" % index)
@@ -119,7 +114,7 @@ def tile_get_qkv_kernel(tc, x_words, x_scales, w_words, w_scales, out_0, out_1, 
                 lhsT=x_codes[g][:, j, :].bitcast(E2M1X4),
                 lhsT_scale=x_planes[g][:, j, :],
                 rhs=w_codes[i][:, g, 2 * c0 : 2 * (c0 + width)].bitcast(E2M1X4),
-                rhs_scale=w_planes[i][:, g, c0 : c0 + width],
+                rhs_scale=(w_first_plane if i == 0 and g == 0 else w_planes[i])[:, g, c0 : c0 + width],
                 start=(g == 0),
                 stop=(g == PASSES - 1),
             )
@@ -143,7 +138,7 @@ def tile_get_qkv_kernel(tc, x_words, x_scales, w_words, w_scales, out_0, out_1, 
         scalar_copy = nc.scalar.copy
 
         first = [(0, [bank(j) for j in range(SETS)]), (512, [bank(SETS + j) for j in range(SETS)])]
-        for half, g in ((0, 0), (1, 0), (0, 1), (1, 1), (0, 2), (1, 2), (0, 3), (1, 3)):
+        for half, g in ((0, 0), (1, 0), (0, 1), (1, 1), (0, 2), (0, 3), (1, 2), (1, 3)):
             c0, accs = first[half]
             for j in range(SETS):
                 multiply(accs[j], 0, c0, 512, j, g)
@@ -152,7 +147,7 @@ def tile_get_qkv_kernel(tc, x_words, x_scales, w_words, w_scales, out_0, out_1, 
             for j in range(SETS):
                 drain(copy, result, accs[j], 512, j)
             store(result, 0, c0, 512)
-        load_planes_by_r(w_planes[2], w_scales, 0, PASSES, 2 * INNER, 3 * INNER)
+        load_w(2, 2, PASSES)
 
         blocks = [(1, 0, 512), (1, 512, 512), (2, 0, 512), (2, 512, 256), (2, 768, 128), (2, 896, 128)]
         for n, (i, c0, width) in enumerate(blocks):

from contextlib import ExitStack

import concourse.mybir as mybir

F32 = mybir.dt.float32
BF16 = mybir.dt.bfloat16
I32 = mybir.dt.int32
U8 = mybir.dt.uint8
E2M1X4 = mybir.dt.float4_e2m1fn_x4

BATCH, POSITIONS, DIM, HEADS, DIM_HEAD = 2, 256, 2048, 16, 64
TOKENS = BATCH * POSITIONS
INNER = HEADS * DIM_HEAD
P = 128
PASSES = DIM // 512
SETS = TOKENS // P
WARM_UP = 9

FLOPS = 2 * TOKENS * DIM * 3 * INNER


def tile_get_qkv_kernel(tc, x_words, x_scales, w_words, w_scales, out_0, out_1, out_2):
    nc = tc.nc
    outs = (out_0, out_1, out_2)

    with ExitStack() as ctx:
        keep = ctx.enter_context(tc.tile_pool(name="keep", bufs=1))
        results = ctx.enter_context(tc.tile_pool(name="results", bufs=4))
        psum = ctx.enter_context(tc.psum_pool(name="psum", bufs=1))
        ctx.enter_context(tc.manual_schedule())

        zeros = keep.tile([P, 512], BF16, name="zeros", align_bytes=256)
        scratch = keep.tile([P, 2], BF16, name="scratch", align_bytes=256)
        x_raw = keep.tile([P, PASSES, 2 * TOKENS], U8, name="x_raw", align_bytes=256)
        xs_raw = keep.tile([P, PASSES, TOKENS], U8, name="xs_raw", align_bytes=256)
        x_codes = [keep.tile([P, SETS, 2 * P], U8, name="x_codes%d" % g, align_bytes=256) for g in range(PASSES)]
        x_planes = [keep.tile([P, SETS, P], U8, name="x_planes%d" % g, align_bytes=256) for g in range(PASSES)]
        w_codes = [keep.tile([P, PASSES, 2 * INNER], U8, name="w_codes%d" % i, align_bytes=256) for i in range(3)]
        w_first_plane = keep.tile([P, 1, INNER], U8, name="w_first_plane", align_bytes=256)
        w_planes = [keep.tile([P, PASSES, INNER], U8, name="w_planes%d" % i, align_bytes=256) for i in range(3)]

        def zero(engine, ap):
            engine.memset(ap.bitcast(I32), 0)

        def load_x(g0, g1):
            nc.sync.dma_start(
                out=x_raw[:, g0:g1, :].bitcast(I32), in_=x_words[g0:g1].rearrange("g p c -> p g c").bitcast(I32)
            )

        def load_w(i, g0, g1, c0=0, c1=INNER):
            cols = slice(2 * (INNER * i + c0), 2 * (INNER * i + c1))
            nc.sync.dma_start(
                out=w_codes[i][:, g0:g1, 2 * c0 : 2 * c1].bitcast(I32),
                in_=w_words[g0:g1, :, cols].rearrange("g p c -> p g c").bitcast(I32),
            )

        def load_planes(planes, scales, g0, g1, c0, c1, rows=(0, 1, 2, 3)):
            for r in rows:
                nc.sync.dma_start(
                    out=planes[r:P:32, g0:g1, :].bitcast(I32),
                    in_=scales[g0:g1, r:16:4, c0:c1].rearrange("g r c -> r g c").bitcast(I32),
                )

        def permute_codes(g):
            nc.vector.tensor_copy(
                out=x_codes[g][:].rearrange("p j (q b e) -> p j q b e", b=BATCH, e=2),
                in_=x_raw[:, g, :].rearrange("p (b q j e) -> p j q b e", b=BATCH, j=SETS, e=2),
            )

        def permute_planes(g):
            nc.vector.tensor_copy(
                out=x_planes[g][:].rearrange("p j (q b) -> p j q b", b=BATCH),
                in_=xs_raw[:, g, :].rearrange("p (b q j) -> p j q b", b=BATCH, j=SETS),
            )

        zero(nc.gpsimd, w_first_plane[:])
        zero(nc.gpsimd, xs_raw[:])
        nc.vector.memset(zeros[:].bitcast(I32), 0)
        zero(nc.vector, w_planes[0][:, 1:PASSES, :])
        zero(nc.gpsimd, w_planes[1][:])
        zero(nc.gpsimd, w_planes[2][:])
        nc.scalar.copy(scratch[:], zeros[:, 0:2])

        load_planes(w_first_plane, w_scales, 0, 1, 0, INNER, (0, 1))
        load_x(0, 1)
        load_planes(xs_raw, x_scales, 0, PASSES, 0, TOKENS, (0, 1, 2, 3))
        load_planes(w_first_plane, w_scales, 0, 1, 0, INNER, (2, 3))
        load_w(0, 0, 1)
        load_x(1, 2)
        load_w(0, 1, 2)
        load_planes(w_planes[0], w_scales, 1, PASSES, 0, INNER)
        load_x(2, PASSES)
        load_w(0, 2, PASSES)
        load_planes(w_planes[1], w_scales, 0, PASSES, INNER, 2 * INNER)
        load_w(1, 0, PASSES)
        load_planes(w_planes[2], w_scales, 0, PASSES, 2 * INNER, 3 * INNER)
        load_w(2, 0, 2)

        for g in range(PASSES):
            permute_codes(g)
            permute_planes(g)

        def bank(index):
            acc = psum.tile([P, 512], F32, name="acc%d" % index)
            return acc

        warm = bank(7)
        for n in range(WARM_UP):
            nc.tensor.matmul(warm[:], lhsT=zeros[:, 0:P], rhs=zeros[:], start=True, stop=True)

        def multiply(acc, i, c0, width, j, g):
            nc.tensor.matmul_mx(
                out=acc[:, 0:width],
                lhsT=x_codes[g][:, j, :].bitcast(E2M1X4),
                lhsT_scale=x_planes[g][:, j, :],
                rhs=w_codes[i][:, g, 2 * c0 : 2 * (c0 + width)].bitcast(E2M1X4),
                rhs_scale=(w_first_plane if i == 0 and g == 0 else w_planes[i])[:, g, c0 : c0 + width],
                start=(g == 0),
                stop=(g == PASSES - 1),
            )

        def result_tile(width):
            result = results.tile([P, width // DIM_HEAD, SETS, DIM_HEAD], F32, name="result%d" % width)
            return result

        def drain(copy, result, acc, width, j):
            copy(out=result[:, :, j, :], in_=acc[:, 0:width].rearrange("p (h d) -> p h d", d=DIM_HEAD))

        def store(result, i, c0, width):
            heads = slice(c0 // DIM_HEAD, (c0 + width) // DIM_HEAD)
            for b in range(BATCH):
                nc.sync.dma_start(
                    out=outs[i][b, heads, :, :].rearrange("h (q j) d -> q h (j d)", j=SETS),
                    in_=result[b:P:BATCH, :, :, :].rearrange("q h j d -> q h (j d)"),
                )

        vector_copy = nc.vector.tensor_copy
        scalar_copy = nc.scalar.copy

        first = [(0, [bank(j) for j in range(SETS)]), (512, [bank(SETS + j) for j in range(SETS)])]
        for half, g in ((0, 0), (1, 0), (0, 1), (1, 1), (0, 2), (0, 3), (1, 2), (1, 3)):
            c0, accs = first[half]
            for j in range(SETS):
                multiply(accs[j], 0, c0, 512, j, g)
        for (c0, accs), copy in zip(first, (scalar_copy, vector_copy)):
            result = result_tile(512)
            for j in range(SETS):
                drain(copy, result, accs[j], 512, j)
            store(result, 0, c0, 512)
        load_w(2, 2, PASSES)

        blocks = [(1, 0, 512), (1, 512, 512), (2, 0, 512), (2, 512, 256), (2, 768, 128), (2, 896, 128)]
        for n, (i, c0, width) in enumerate(blocks):
            result = result_tile(width)
            for j in range(SETS):
                acc = bank(SETS * (n % 2) + j)
                for g in range(PASSES):
                    multiply(acc, i, c0, width, j, g)
                drain((scalar_copy, vector_copy)[n % 2], result, acc, width, j)
            store(result, i, c0, width)
